import numpy as np
import ml_dtypes


def mxq(x, axis, fmt="e4m3"):
    dtype, down = {"e4m3": (ml_dtypes.float8_e4m3fn, 7), "e5m2": (ml_dtypes.float8_e5m2, 14)}[fmt]
    v = np.moveaxis(np.asarray(x, np.float32).astype(ml_dtypes.bfloat16).astype(np.float64), axis, -1)
    blocks = v.reshape(v.shape[:-1] + (-1, 32))
    amax = np.abs(blocks).max(-1, keepdims=True)
    byte = np.maximum(np.where(amax > 0, np.frexp(amax)[1] - 1 + 127, 0) - down, 1)
    scale = np.exp2(byte - 127.0)
    codes = (blocks / scale).astype(np.float32).astype(dtype).astype(np.float64)
    return np.moveaxis((codes * scale).reshape(v.shape), -1, axis)


WIDE = False


def mx_kscale(k):
    if not WIDE:
        return np.ones(k)
    levels = np.array([10, -10, 5, -5, 0])
    a = np.random.permutation(np.resize(levels, k // 512 * 4)).reshape(k // 512, 4)
    idx = np.arange(k)
    return np.exp2(a[idx // 512, idx % 128 // 32])


BF16 = ml_dtypes.bfloat16


def bf(x):
    return np.asarray(x, np.float32).astype(BF16)


def f64(x):
    return np.asarray(x).astype(np.float64)


E2M1 = np.array([0.0, 0.5, 1.0, 1.5, 2.0, 3.0, 4.0, 6.0, -0.0, -0.5, -1.0, -1.5, -2.0, -3.0, -4.0, -6.0])


def pack_weight(w, fmt):
    k, n = w.shape
    w = f64(bf(w)).reshape(k // 32, 32, n)
    amax = np.abs(w).max(1)
    if fmt == "e4m3":
        byte = np.frexp(amax)[1] - 1 + 127 - 7
    else:
        mant, ex = np.frexp(amax / 6.0)
        byte = np.where(mant > 0.5, ex, ex - 1) + 127
    byte = np.clip(np.where(amax > 0, byte, 1), 1, 254)
    scaled = (w * np.exp2(127.0 - byte)[:, None, :]).reshape(k, n).astype(np.float32)
    by_word = np.ascontiguousarray(scaled.reshape(k // 512, 128, 4, n).transpose(0, 1, 3, 2))
    if fmt == "e4m3":
        words = by_word.astype(ml_dtypes.float8_e4m3fn).view(np.uint8)
    else:
        c = by_word.astype(ml_dtypes.float4_e2m1fn).view(np.uint8) & 0xF
        words = c[..., 0::2] | (c[..., 1::2] << 4)
    return np.ascontiguousarray(words), np.ascontiguousarray(byte.astype(np.uint8).reshape(k // 512, 16, n))


def unpack_weight(words, scales, fmt):
    g, p, n, _ = words.shape
    if fmt == "e4m3":
        vals = np.ascontiguousarray(words).view(ml_dtypes.float8_e4m3fn).astype(np.float64)
    else:
        nib = np.empty((g, p, n, 4), np.uint8)
        nib[..., 0::2] = words & 0xF
        nib[..., 1::2] = words >> 4
        vals = E2M1[nib]
    vals = vals * np.repeat(np.exp2(scales.astype(np.float64) - 127.0), 8, axis=1)[..., None]
    return vals.transpose(0, 1, 3, 2).reshape(g * 512, n)


B, C, PS, G, E = 24, 3, 64, 4, 512
NP = G * G
K2 = 2 * E
FMT = "e4m3"


def setup_inputs():
    s = mx_kscale(K2)[:E]
    t = mx_kscale(K2)[:E]
    ss = np.concatenate([s, s])
    tt = np.concatenate([t, t])
    tok = bf(np.random.standard_normal((B, NP, E)) * s)
    corr_w = np.random.standard_normal((E, K2)) / np.sqrt(K2) * t[:, None] / ss[None, :]
    corr_w_words, corr_w_scales = pack_weight(np.ascontiguousarray(corr_w.T), FMT)
    corr_b = bf(np.random.standard_normal(E) * 0.3 * t)
    cross_w = np.random.standard_normal((E, K2)) / np.sqrt(K2) / tt[None, :]
    cross_w_words, cross_w_scales = pack_weight(np.ascontiguousarray(cross_w.T), FMT)
    cross_b = bf(np.random.standard_normal(E) * 0.3)
    return {"tok": tok,
            "corr_w_words": corr_w_words,
            "corr_w_scales": corr_w_scales,
            "corr_b": corr_b,
            "cross_w_words": cross_w_words,
            "cross_w_scales": cross_w_scales,
            "cross_b": cross_b}


def reference(tok, corr_w_words, corr_w_scales, corr_b, cross_w_words, cross_w_scales, cross_b):
    xc = f64(tok)
    a = np.broadcast_to(xc[:, :, None, :], (B, NP, NP, E))
    b = np.broadcast_to(xc[:, None, :, :], (B, NP, NP, E))
    cart = np.concatenate([a, b], axis=-1)
    h = (mxq(cart, 3, "e4m3") @ unpack_weight(corr_w_words, corr_w_scales, FMT)) + f64(corr_b)
    h = h.reshape(B, NP, NP // 2, K2)
    return (mxq(h, 3, "e4m3") @ unpack_weight(cross_w_words, cross_w_scales, FMT)) + f64(cross_b)

@@ -1,0 +1,209 @@
+from contextlib import ExitStack
+
+import concourse.mybir as mybir
+from concourse.masks import make_identity
+
+F32 = mybir.dt.float32
+BF16 = mybir.dt.bfloat16
+I32 = mybir.dt.int32
+U32 = mybir.dt.uint32
+U8 = mybir.dt.uint8
+FP8X4 = mybir.dt.float8_e4m3fn_x4
+ADD = mybir.AluOpType.add
+IDENTITY = mybir.ActivationFunctionType.Identity
+
+P = 128
+PACK = 4
+BATCH, TOKENS, EMBED = 24, 16, 512
+PAIRS = TOKENS // 2
+HALVES = 2
+TOKEN_TILES = BATCH * TOKENS // P
+IMAGES_PER_TILE = P // TOKENS
+BLOCK_IMAGES = 4
+BLOCKS = BATCH // BLOCK_IMAGES
+BLOCK_ROWS = BLOCK_IMAGES * TOKENS * PAIRS
+OUT_TILES = EMBED // P
+
+FLOPS = 2 * BATCH * TOKENS * TOKENS * (2 * EMBED) * EMBED + 2 * BATCH * TOKENS * PAIRS * (2 * EMBED) * EMBED
+
+
+def tile_simplemodel_pb_kernel(
+    tc, tok, corr_w_words, corr_w_scales, corr_b, cross_w_words, cross_w_scales, cross_b, out
+):
+    nc = tc.nc
+    tok_rows = tok.rearrange("b i e -> (b i) e")
+    out_rows = out.rearrange("b i m n -> (b i m) n")
+
+    with ExitStack() as ctx:
+        keep = ctx.enter_context(tc.tile_pool(name="keep", bufs=1))
+        row_pool = ctx.enter_context(tc.tile_pool(name="row_pool", bufs=4))
+        h_pool = ctx.enter_context(tc.tile_pool(name="h_pool", bufs=3))
+        g_pool = ctx.enter_context(tc.tile_pool(name="g_pool", bufs=4))
+        out_pool = ctx.enter_context(tc.tile_pool(name="out_pool", bufs=2))
+        psum = ctx.enter_context(tc.psum_pool(name="psum", bufs=4))
+        ctx.enter_context(tc.manual_schedule())
+
+        planes = keep.tile([P, 2 * HALVES, EMBED], U8, align_bytes=64)
+        nc.vector.memset(planes[:].bitcast(I32), 0)
+        ident = keep.tile([P, P], F32)
+        make_identity(nc, ident[:])
+
+        tok_sb = keep.tile([P, TOKEN_TILES, EMBED], BF16)
+        for a in range(TOKEN_TILES):
+            nc.sync.dma_start(out=tok_sb[:, a, :], in_=tok_rows[a * P : (a + 1) * P, :])
+
+        def load_weight(words_dram, scales_dram, words_sb, first_plane):
+            scale_rows = scales_dram.bitcast(I32).rearrange("g (q r) n -> r q g n", r=4)
+            for r in range(4):
+                nc.sync.dma_start(
+                    out=planes[r:P:32, first_plane : first_plane + HALVES, :].bitcast(I32), in_=scale_rows[r]
+                )
+            nc.sync.dma_start(
+                out=words_sb[:].bitcast(I32), in_=words_dram.rearrange("g p n t -> p g (n t)").bitcast(I32)
+            )
+
+        corr_words = keep.tile([P, HALVES, PACK * EMBED], U8, align_bytes=64)
+        cross_words = keep.tile([P, HALVES, PACK * EMBED], U8, align_bytes=64)
+        load_weight(corr_w_words, corr_w_scales, corr_words, 0)
+        corr_b_bf = keep.tile([P, PACK], BF16)
+        nc.sync.dma_start(out=corr_b_bf[:], in_=corr_b.rearrange("(p t) -> p t", t=PACK))
+        load_weight(cross_w_words, cross_w_scales, cross_words, HALVES)
+        cross_b_bf = keep.tile([P, OUT_TILES], BF16)
+        with nc.allow_non_contiguous_dma(reason="512 bias values, one to a partition and output tile"):
+            nc.sync.dma_start(out=cross_b_bf[:], in_=cross_b.rearrange("(c m) -> m c", m=P))
+
+        tok_grouped = keep.tile([P, TOKEN_TILES, PACK * P], BF16, align_bytes=64)
+        tok_codes = keep.tile([P, TOKEN_TILES, P], U32, align_bytes=64)
+        tok_scales = keep.tile([P, TOKEN_TILES, P], U8, align_bytes=64)
+        for a in range(TOKEN_TILES):
+            pair_words = tok_sb[:, a, :].bitcast(F32)
+            tok_t = psum.tile([P, 2, P], F32, tag="tr")
+            for u in range(2):
+                nc.tensor.transpose(out=tok_t[:, u, :], in_=pair_words[:, u : EMBED // 2 : 2], identity=ident[:])
+            nc.vector.tensor_copy(
+                out=tok_grouped[:, a, :].bitcast(F32).rearrange("p (k u) -> p k u", u=2),
+                in_=tok_t[:].rearrange("p u k -> p k u"),
+            )
+            nc.vector.quantize_mx(
+                out=tok_codes[:, a, :].bitcast(FP8X4), scales=tok_scales[:, a, :], in_=tok_grouped[:, a, :]
+            )
+
+        left_t = keep.tile([P, BATCH * TOKENS, PACK], F32)
+        right_t = keep.tile([P, HALVES, BATCH, PAIRS, PACK], F32)
+        corr_b_f = keep.tile([P, PACK], F32)
+        cross_b_f = keep.tile([P, OUT_TILES], F32)
+        token_rows = {}
+        flipped = {}
+
+        def first_matmul(a):
+            for half in range(HALVES):
+                sums = psum.tile([P, EMBED], F32, tag="mx")
+                nc.tensor.matmul_mx(
+                    out=sums[:],
+                    lhsT=tok_codes[:, a, :].bitcast(FP8X4),
+                    lhsT_scale=tok_scales[:, a, :],
+                    rhs=corr_words[:, half, :].bitcast(FP8X4),
+                    rhs_scale=planes[:, half, :],
+                    start=True,
+                    stop=True,
+                )
+                rows = row_pool.tile([P, PACK, P], F32, tag="rows")
+                nc.scalar.copy(out=rows[:], in_=sums[:].rearrange("k (p t) -> k t p", t=PACK))
+                token_rows[(a, half)] = rows
+
+        def flip_back(a):
+            for half in range(HALVES):
+                flip = psum.tile([P, PACK, P], F32, tag="tr")
+                for t in range(PACK):
+                    nc.tensor.transpose(out=flip[:, t, :], in_=token_rows[(a, half)][:, t, :], identity=ident[:])
+                flipped[(a, half)] = flip
+            by_parity = flipped[(a, 1)][:].rearrange("p t (q j) -> p j q t", j=HALVES)
+            images = slice(a * IMAGES_PER_TILE, (a + 1) * IMAGES_PER_TILE)
+            for parity in range(HALVES):
+                nc.scalar.copy(
+                    out=right_t[:, parity, images, :, :].rearrange("p b m t -> p (b m) t"), in_=by_parity[:, parity]
+                )
+
+        def add_first_bias(a):
+            nc.vector.tensor_tensor(
+                out=left_t[:, a * P : (a + 1) * P, :],
+                in0=flipped[(a, 0)][:].rearrange("p t k -> p k t"),
+                in1=corr_b_f[:].unsqueeze(1).to_broadcast([P, P, PACK]),
+                op=ADD,
+            )
+
+        first_matmul(0)
+        first_matmul(1)
+        flip_back(0)
+        nc.vector.tensor_copy(out=corr_b_f[:], in_=corr_b_bf[:])
+        add_first_bias(0)
+        first_matmul(2)
+        flip_back(1)
+        flip_back(2)
+
+        shape = [P, BLOCK_IMAGES, TOKENS, PAIRS, PACK]
+        h_of = {}
+        out_t_psum = {}
+
+        def pair_sums(block, parity):
+            h = h_pool.tile([P, BLOCK_ROWS * PACK], BF16, tag="h", align_bytes=64)
+            tokens = slice(block * BLOCK_IMAGES * TOKENS, (block + 1) * BLOCK_IMAGES * TOKENS)
+            images = slice(block * BLOCK_IMAGES, (block + 1) * BLOCK_IMAGES)
+            nc.vector.tensor_tensor(
+                out=h[:].rearrange("p (b i m t) -> p b i m t", b=BLOCK_IMAGES, i=TOKENS, m=PAIRS),
+                in0=left_t[:, tokens, :].rearrange("p (b i) t -> p b i t", b=BLOCK_IMAGES).unsqueeze(3).to_broadcast(shape),
+                in1=right_t[:, parity, images, :, :].unsqueeze(2).to_broadcast(shape),
+                op=ADD,
+            )
+            h_of[(block, parity)] = h
+
+        def second_matmul_pass(block, parity):
+            codes = g_pool.tile([P, BLOCK_ROWS], U32, tag="codes", align_bytes=64)
+            scales = g_pool.tile([P, BLOCK_ROWS], U8, tag="scales", align_bytes=64)
+            nc.vector.quantize_mx(out=codes[:].bitcast(FP8X4), scales=scales[:], in_=h_of[(block, parity)][:])
+            for c in range(OUT_TILES):
+                if parity == 0:
+                    out_t_psum[c] = psum.tile([P, BLOCK_ROWS], F32, tag="mx", name="out_t_psum%d" % c)
+                nc.tensor.matmul_mx(
+                    out=out_t_psum[c][:],
+                    lhsT=cross_words[:, parity, c * PACK * P : (c + 1) * PACK * P].bitcast(FP8X4),
+                    lhsT_scale=planes[:, HALVES + parity, c * P : (c + 1) * P],
+                    rhs=codes[:].bitcast(FP8X4),
+                    rhs_scale=scales[:],
+                    start=(parity == 0),
+                    stop=(parity == HALVES - 1),
+                )
+
+        def finish_block(block):
+            out_t = out_pool.tile([P, OUT_TILES, BLOCK_ROWS], F32, tag="out_t")
+            result = out_pool.tile([P, BLOCK_IMAGES, EMBED], F32, tag="result")
+            row_psum = {}
+            for image in range(BLOCK_IMAGES):
+                row_psum[image] = psum.tile([P, EMBED], F32, tag="tr", name="row_psum%d" % image)
+            for c in range(OUT_TILES):
+                nc.scalar.activation(
+                    out=out_t[:, c, :], in_=out_t_psum[c][:], func=IDENTITY, bias=cross_b_f[:, c : c + 1], scale=1.0
+                )
+                for image in range(BLOCK_IMAGES):
+                    nc.tensor.transpose(
+                        out=row_psum[image][:, c * P : (c + 1) * P],
+                        in_=out_t[:, c, image * P : (image + 1) * P],
+                        identity=ident[:],
+                    )
+            for image in range(BLOCK_IMAGES):
+                nc.scalar.copy(out=result[:, image, :], in_=row_psum[image][:])
+                first_row = (block * BLOCK_IMAGES + image) * P
+                nc.sync.dma_start(out=out_rows[first_row : first_row + P, :], in_=result[:, image, :])
+
+        units = [(block, parity) for block in range(BLOCKS) for parity in range(HALVES)]
+        for u in range(len(units) + 1):
+            if u < len(units):
+                pair_sums(units[u][0], units[u][1])
+            if u == 1:
+                nc.vector.tensor_copy(out=cross_b_f[:], in_=cross_b_bf[:])
+            if 0 < u < TOKEN_TILES:
+                add_first_bias(u)
+            if u > 0:
+                second_matmul_pass(units[u - 1][0], units[u - 1][1])
+                if units[u - 1][1] == HALVES - 1:
+                    finish_block(units[u - 1][0])

@@ -49,7 +49,8 @@ def tile_simplemodel_pb_kernel(
         make_identity(nc, ident[:])
 
         tok_sb = keep.tile([P, TOKEN_TILES, EMBED], BF16)
-        for a in range(TOKEN_TILES):
+
+        def load_tokens(a):
             nc.sync.dma_start(out=tok_sb[:, a, :], in_=tok_rows[a * P : (a + 1) * P, :])
 
         def load_weight(words_dram, scales_dram, words_sb, first_plane):
@@ -64,7 +65,10 @@ def tile_simplemodel_pb_kernel(
 
         corr_words = keep.tile([P, HALVES, PACK * EMBED], U8, align_bytes=64)
         cross_words = keep.tile([P, HALVES, PACK * EMBED], U8, align_bytes=64)
+        load_tokens(0)
         load_weight(corr_w_words, corr_w_scales, corr_words, 0)
+        load_tokens(1)
+        load_tokens(2)
         corr_b_bf = keep.tile([P, PACK], BF16)
         nc.sync.dma_start(out=corr_b_bf[:], in_=corr_b.rearrange("(p t) -> p t", t=PACK))
         load_weight(cross_w_words, cross_w_scales, cross_words, HALVES)
@@ -75,7 +79,8 @@ def tile_simplemodel_pb_kernel(
         tok_grouped = keep.tile([P, TOKEN_TILES, PACK * P], BF16, align_bytes=64)
         tok_codes = keep.tile([P, TOKEN_TILES, P], U32, align_bytes=64)
         tok_scales = keep.tile([P, TOKEN_TILES, P], U8, align_bytes=64)
-        for a in range(TOKEN_TILES):
+
+        def quantise_tokens(a):
             pair_words = tok_sb[:, a, :].bitcast(F32)
             tok_t = psum.tile([P, 2, P], F32, tag="tr")
             for u in range(2):
@@ -132,11 +137,14 @@ def tile_simplemodel_pb_kernel(
                 op=ADD,
             )
 
+        quantise_tokens(0)
         first_matmul(0)
-        first_matmul(1)
+        quantise_tokens(1)
+        quantise_tokens(2)
         flip_back(0)
         nc.vector.tensor_copy(out=corr_b_f[:], in_=corr_b_bf[:])
         add_first_bias(0)
+        first_matmul(1)
         first_matmul(2)
         flip_back(1)
         flip_back(2)
@@ -180,10 +188,14 @@ def tile_simplemodel_pb_kernel(
             row_psum = {}
             for image in range(BLOCK_IMAGES):
                 row_psum[image] = psum.tile([P, EMBED], F32, tag="tr", name="row_psum%d" % image)
+            vector_helps = block == BLOCKS - 1
             for c in range(OUT_TILES):
-                nc.scalar.activation(
-                    out=out_t[:, c, :], in_=out_t_psum[c][:], func=IDENTITY, bias=cross_b_f[:, c : c + 1], scale=1.0
-                )
+                if vector_helps and c % 2 == 1:
+                    nc.vector.tensor_scalar_add(out=out_t[:, c, :], in0=out_t_psum[c][:], scalar1=cross_b_f[:, c : c + 1])
+                else:
+                    nc.scalar.activation(
+                        out=out_t[:, c, :], in_=out_t_psum[c][:], func=IDENTITY, bias=cross_b_f[:, c : c + 1], scale=1.0
+                    )
                 for image in range(BLOCK_IMAGES):
                     nc.tensor.transpose(
                         out=row_psum[image][:, c * P : (c + 1) * P],
@@ -191,7 +203,10 @@ def tile_simplemodel_pb_kernel(
                         identity=ident[:],
                     )
             for image in range(BLOCK_IMAGES):
-                nc.scalar.copy(out=result[:, image, :], in_=row_psum[image][:])
+                if vector_helps and image % 2 == 1:
+                    nc.vector.tensor_copy(out=result[:, image, :], in_=row_psum[image][:])
+                else:
+                    nc.scalar.copy(out=result[:, image, :], in_=row_psum[image][:])
                 first_row = (block * BLOCK_IMAGES + image) * P
                 nc.sync.dma_start(out=out_rows[first_row : first_row + P, :], in_=result[:, image, :])
 

@@ -22,6 +22,7 @@ IMAGES_PER_TILE = P // TOKENS
 BLOCK_IMAGES = 4
 BLOCKS = BATCH // BLOCK_IMAGES
 BLOCK_ROWS = BLOCK_IMAGES * TOKENS * PAIRS
+HALF_ROWS = BLOCK_ROWS // 2
 OUT_TILES = EMBED // P
 
 FLOPS = 2 * BATCH * TOKENS * TOKENS * (2 * EMBED) * EMBED + 2 * BATCH * TOKENS * PAIRS * (2 * EMBED) * EMBED
@@ -49,8 +50,7 @@ def tile_simplemodel_pb_kernel(
         make_identity(nc, ident[:])
 
         tok_sb = keep.tile([P, TOKEN_TILES, EMBED], BF16)
-
-        def load_tokens(a):
+        for a in range(TOKEN_TILES):
             nc.sync.dma_start(out=tok_sb[:, a, :], in_=tok_rows[a * P : (a + 1) * P, :])
 
         def load_weight(words_dram, scales_dram, words_sb, first_plane):
@@ -65,22 +65,17 @@ def tile_simplemodel_pb_kernel(
 
         corr_words = keep.tile([P, HALVES, PACK * EMBED], U8, align_bytes=64)
         cross_words = keep.tile([P, HALVES, PACK * EMBED], U8, align_bytes=64)
-        load_tokens(0)
         load_weight(corr_w_words, corr_w_scales, corr_words, 0)
-        load_tokens(1)
-        load_tokens(2)
         corr_b_bf = keep.tile([P, PACK], BF16)
         nc.sync.dma_start(out=corr_b_bf[:], in_=corr_b.rearrange("(p t) -> p t", t=PACK))
         load_weight(cross_w_words, cross_w_scales, cross_words, HALVES)
-        cross_b_bf = keep.tile([P, OUT_TILES], BF16)
-        with nc.allow_non_contiguous_dma(reason="512 bias values, one to a partition and output tile"):
-            nc.sync.dma_start(out=cross_b_bf[:], in_=cross_b.rearrange("(c m) -> m c", m=P))
+        cross_b_rows_bf = keep.tile([P, EMBED], BF16)
+        nc.sync.dma_start(out=cross_b_rows_bf[:], in_=cross_b.partition_broadcast(P))
 
         tok_grouped = keep.tile([P, TOKEN_TILES, PACK * P], BF16, align_bytes=64)
         tok_codes = keep.tile([P, TOKEN_TILES, P], U32, align_bytes=64)
         tok_scales = keep.tile([P, TOKEN_TILES, P], U8, align_bytes=64)
-
-        def quantise_tokens(a):
+        for a in range(TOKEN_TILES):
             pair_words = tok_sb[:, a, :].bitcast(F32)
             tok_t = psum.tile([P, 2, P], F32, tag="tr")
             for u in range(2):
@@ -97,6 +92,7 @@ def tile_simplemodel_pb_kernel(
         right_t = keep.tile([P, HALVES, BATCH, PAIRS, PACK], F32)
         corr_b_f = keep.tile([P, PACK], F32)
         cross_b_f = keep.tile([P, OUT_TILES], F32)
+        cross_b_rows = keep.tile([P, EMBED], F32)
         token_rows = {}
         flipped = {}
 
@@ -137,10 +133,14 @@ def tile_simplemodel_pb_kernel(
                 op=ADD,
             )
 
-        quantise_tokens(0)
+        def spread_second_bias():
+            nc.scalar.copy(out=cross_b_rows[:], in_=cross_b_rows_bf[:])
+            bias_t = psum.tile([P, OUT_TILES, P], F32, tag="tr")
+            for c in range(OUT_TILES):
+                nc.tensor.transpose(out=bias_t[:, c, :], in_=cross_b_rows[:, c * P : (c + 1) * P], identity=ident[:])
+            nc.scalar.copy(out=cross_b_f[:], in_=bias_t[:, :, 0])
+
         first_matmul(0)
-        quantise_tokens(1)
-        quantise_tokens(2)
         flip_back(0)
         nc.vector.tensor_copy(out=corr_b_f[:], in_=corr_b_bf[:])
         add_first_bias(0)
@@ -172,53 +172,70 @@ def tile_simplemodel_pb_kernel(
             for c in range(OUT_TILES):
                 if parity == 0:
                     out_t_psum[c] = psum.tile([P, BLOCK_ROWS], F32, tag="mx", name="out_t_psum%d" % c)
-                nc.tensor.matmul_mx(
-                    out=out_t_psum[c][:],
-                    lhsT=cross_words[:, parity, c * PACK * P : (c + 1) * PACK * P].bitcast(FP8X4),
-                    lhsT_scale=planes[:, HALVES + parity, c * P : (c + 1) * P],
-                    rhs=codes[:].bitcast(FP8X4),
-                    rhs_scale=scales[:],
-                    start=(parity == 0),
-                    stop=(parity == HALVES - 1),
-                )
+                weight_columns = cross_words[:, parity, c * PACK * P : (c + 1) * PACK * P]
+                weight_scales = planes[:, HALVES + parity, c * P : (c + 1) * P]
+                if block < BLOCKS - 1:
+                    nc.tensor.matmul_mx(
+                        out=out_t_psum[c][:],
+                        lhsT=weight_columns.bitcast(FP8X4),
+                        lhsT_scale=weight_scales,
+                        rhs=codes[:].bitcast(FP8X4),
+                        rhs_scale=scales[:],
+                        start=(parity == 0),
+                        stop=(parity == HALVES - 1),
+                    )
+                else:
+                    nc.tensor.matmul_mx(
+                        out=out_t_psum[c][:],
+                        lhsT=codes[:, c * P : (c + 1) * P].bitcast(FP8X4),
+                        lhsT_scale=scales[:, c * P : (c + 1) * P],
+                        rhs=cross_words[:, parity, :].bitcast(FP8X4),
+                        rhs_scale=planes[:, HALVES + parity, :],
+                        start=(parity == 0),
+                        stop=(parity == HALVES - 1),
+                    )
+
+        def finish_last_block(block):
+            result = out_pool.tile([P, BLOCK_IMAGES, EMBED], F32, tag="result")
+            for image in range(BLOCK_IMAGES):
+                nc.vector.tensor_tensor(out=result[:, image, :], in0=out_t_psum[image][:], in1=cross_b_rows[:], op=ADD)
+                first_out_row = (block * BLOCK_IMAGES + image) * P
+                nc.sync.dma_start(out=out_rows[first_out_row : first_out_row + P, :], in_=result[:, image, :])
 
         def finish_block(block):
             out_t = out_pool.tile([P, OUT_TILES, BLOCK_ROWS], F32, tag="out_t")
             result = out_pool.tile([P, BLOCK_IMAGES, EMBED], F32, tag="result")
-            row_psum = {}
-            for image in range(BLOCK_IMAGES):
-                row_psum[image] = psum.tile([P, EMBED], F32, tag="tr", name="row_psum%d" % image)
-            vector_helps = block == BLOCKS - 1
-            for c in range(OUT_TILES):
-                if vector_helps and c % 2 == 1:
-                    nc.vector.tensor_scalar_add(out=out_t[:, c, :], in0=out_t_psum[c][:], scalar1=cross_b_f[:, c : c + 1])
-                else:
+            for first_row in range(0, BLOCK_ROWS, HALF_ROWS):
+                for c in range(OUT_TILES):
                     nc.scalar.activation(
-                        out=out_t[:, c, :], in_=out_t_psum[c][:], func=IDENTITY, bias=cross_b_f[:, c : c + 1], scale=1.0
-                    )
-                for image in range(BLOCK_IMAGES):
-                    nc.tensor.transpose(
-                        out=row_psum[image][:, c * P : (c + 1) * P],
-                        in_=out_t[:, c, image * P : (image + 1) * P],
-                        identity=ident[:],
+                        out=out_t[:, c, first_row : first_row + HALF_ROWS],
+                        in_=out_t_psum[c][:, first_row : first_row + HALF_ROWS],
+                        func=IDENTITY,
+                        bias=cross_b_f[:, c : c + 1],
+                        scale=1.0,
                     )
             for image in range(BLOCK_IMAGES):
-                if vector_helps and image % 2 == 1:
-                    nc.vector.tensor_copy(out=result[:, image, :], in_=row_psum[image][:])
-                else:
-                    nc.scalar.copy(out=result[:, image, :], in_=row_psum[image][:])
-                first_row = (block * BLOCK_IMAGES + image) * P
-                nc.sync.dma_start(out=out_rows[first_row : first_row + P, :], in_=result[:, image, :])
+                rows = psum.tile([P, EMBED], F32, tag="tr")
+                for c in range(OUT_TILES):
+                    nc.tensor.transpose(
+                        out=rows[:, c * P : (c + 1) * P], in_=out_t[:, c, image * P : (image + 1) * P], identity=ident[:]
+                    )
+                nc.scalar.copy(out=result[:, image, :], in_=rows[:])
+                first_out_row = (block * BLOCK_IMAGES + image) * P
+                nc.sync.dma_start(out=out_rows[first_out_row : first_out_row + P, :], in_=result[:, image, :])
 
         units = [(block, parity) for block in range(BLOCKS) for parity in range(HALVES)]
         for u in range(len(units) + 1):
             if u < len(units):
                 pair_sums(units[u][0], units[u][1])
-            if u == 1:
-                nc.vector.tensor_copy(out=cross_b_f[:], in_=cross_b_bf[:])
             if 0 < u < TOKEN_TILES:
                 add_first_bias(u)
+            if u == 1:
+                spread_second_bias()
             if u > 0:
                 second_matmul_pass(units[u - 1][0], units[u - 1][1])
                 if units[u - 1][1] == HALVES - 1:
-                    finish_block(units[u - 1][0])
+                    if units[u - 1][0] < BLOCKS - 1:
+                        finish_block(units[u - 1][0])
+                    else:
+                        finish_last_block(units[u - 1][0])

@@ -23,6 +23,9 @@ BLOCK_IMAGES = 4
 BLOCKS = BATCH // BLOCK_IMAGES
 BLOCK_ROWS = BLOCK_IMAGES * TOKENS * PAIRS
 HALF_ROWS = BLOCK_ROWS // 2
+VECTOR_IMAGES = BLOCK_IMAGES - 1
+IMAGE_COLUMNS = TOKENS * PAIRS * PACK
+DIRECT_BLOCKS = 3
 OUT_TILES = EMBED // P
 
 FLOPS = 2 * BATCH * TOKENS * TOKENS * (2 * EMBED) * EMBED + 2 * BATCH * TOKENS * PAIRS * (2 * EMBED) * EMBED
@@ -39,9 +42,11 @@ def tile_simplemodel_pb_kernel(
         keep = ctx.enter_context(tc.tile_pool(name="keep", bufs=1))
         row_pool = ctx.enter_context(tc.tile_pool(name="row_pool", bufs=4))
         h_pool = ctx.enter_context(tc.tile_pool(name="h_pool", bufs=3))
-        g_pool = ctx.enter_context(tc.tile_pool(name="g_pool", bufs=4))
+        g_pool = ctx.enter_context(tc.tile_pool(name="g_pool", bufs=DIRECT_BLOCKS * HALVES))
         out_pool = ctx.enter_context(tc.tile_pool(name="out_pool", bufs=2))
-        psum = ctx.enter_context(tc.psum_pool(name="psum", bufs=4))
+        psum_left = ctx.enter_context(tc.psum_pool(name="psum_left", bufs=TOKEN_TILES))
+        psum_mx = ctx.enter_context(tc.psum_pool(name="psum_mx", bufs=3))
+        psum_tr = ctx.enter_context(tc.psum_pool(name="psum_tr", bufs=2))
         ctx.enter_context(tc.manual_schedule())
 
         planes = keep.tile([P, 2 * HALVES, EMBED], U8, align_bytes=64)
@@ -77,7 +82,7 @@ def tile_simplemodel_pb_kernel(
         tok_scales = keep.tile([P, TOKEN_TILES, P], U8, align_bytes=64)
         for a in range(TOKEN_TILES):
             pair_words = tok_sb[:, a, :].bitcast(F32)
-            tok_t = psum.tile([P, 2, P], F32, tag="tr")
+            tok_t = psum_tr.tile([P, 2, P], F32, tag="tr")
             for u in range(2):
                 nc.tensor.transpose(out=tok_t[:, u, :], in_=pair_words[:, u : EMBED // 2 : 2], identity=ident[:])
             nc.vector.tensor_copy(
@@ -88,17 +93,18 @@ def tile_simplemodel_pb_kernel(
                 out=tok_codes[:, a, :].bitcast(FP8X4), scales=tok_scales[:, a, :], in_=tok_grouped[:, a, :]
             )
 
-        left_t = keep.tile([P, BATCH * TOKENS, PACK], F32)
+        left_fourth = keep.tile([P, BLOCKS, TOKENS, PACK], F32)
         right_t = keep.tile([P, HALVES, BATCH, PAIRS, PACK], F32)
         corr_b_f = keep.tile([P, PACK], F32)
         cross_b_f = keep.tile([P, OUT_TILES], F32)
         cross_b_rows = keep.tile([P, EMBED], F32)
         token_rows = {}
-        flipped = {}
+        left_psum = {}
+        right_psum = {}
 
         def first_matmul(a):
             for half in range(HALVES):
-                sums = psum.tile([P, EMBED], F32, tag="mx")
+                sums = psum_mx.tile([P, EMBED], F32, tag="mx")
                 nc.tensor.matmul_mx(
                     out=sums[:],
                     lhsT=tok_codes[:, a, :].bitcast(FP8X4),
@@ -113,29 +119,34 @@ def tile_simplemodel_pb_kernel(
                 token_rows[(a, half)] = rows
 
         def flip_back(a):
-            for half in range(HALVES):
-                flip = psum.tile([P, PACK, P], F32, tag="tr")
-                for t in range(PACK):
-                    nc.tensor.transpose(out=flip[:, t, :], in_=token_rows[(a, half)][:, t, :], identity=ident[:])
-                flipped[(a, half)] = flip
-            by_parity = flipped[(a, 1)][:].rearrange("p t (q j) -> p j q t", j=HALVES)
-            images = slice(a * IMAGES_PER_TILE, (a + 1) * IMAGES_PER_TILE)
-            for parity in range(HALVES):
-                nc.scalar.copy(
-                    out=right_t[:, parity, images, :, :].rearrange("p b m t -> p (b m) t"), in_=by_parity[:, parity]
-                )
+            left = psum_left.tile([P, PACK, P], F32, tag="left")
+            right = psum_tr.tile([P, PACK, P], F32, tag="tr")
+            for t in range(PACK):
+                nc.tensor.transpose(out=right[:, t, :], in_=token_rows[(a, 1)][:, t, :], identity=ident[:])
+            for t in range(PACK):
+                nc.tensor.transpose(out=left[:, t, :], in_=token_rows[(a, 0)][:, t, :], identity=ident[:])
+            left_psum[a] = left
+            right_psum[a] = right
+            blocks_of_tile = IMAGES_PER_TILE // BLOCK_IMAGES
+            nc.scalar.copy(
+                out=left_fourth[:, a * blocks_of_tile : (a + 1) * blocks_of_tile, :, :],
+                in_=left[:].rearrange("p t (b i) -> p b i t", i=TOKENS)[:, VECTOR_IMAGES:IMAGES_PER_TILE:BLOCK_IMAGES],
+            )
 
         def add_first_bias(a):
-            nc.vector.tensor_tensor(
-                out=left_t[:, a * P : (a + 1) * P, :],
-                in0=flipped[(a, 0)][:].rearrange("p t k -> p k t"),
-                in1=corr_b_f[:].unsqueeze(1).to_broadcast([P, P, PACK]),
-                op=ADD,
-            )
+            by_parity = right_psum[a][:].rearrange("p t (q j) -> p j q t", j=HALVES)
+            images = slice(a * IMAGES_PER_TILE, (a + 1) * IMAGES_PER_TILE)
+            for parity in range(HALVES):
+                nc.vector.tensor_tensor(
+                    out=right_t[:, parity, images, :, :].rearrange("p b m t -> p (b m) t"),
+                    in0=by_parity[:, parity],
+                    in1=corr_b_f[:].unsqueeze(1).to_broadcast([P, IMAGES_PER_TILE * PAIRS, PACK]),
+                    op=ADD,
+                )
 
         def spread_second_bias():
             nc.scalar.copy(out=cross_b_rows[:], in_=cross_b_rows_bf[:])
-            bias_t = psum.tile([P, OUT_TILES, P], F32, tag="tr")
+            bias_t = psum_tr.tile([P, OUT_TILES, P], F32, tag="tr")
             for c in range(OUT_TILES):
                 nc.tensor.transpose(out=bias_t[:, c, :], in_=cross_b_rows[:, c * P : (c + 1) * P], identity=ident[:])
             nc.scalar.copy(out=cross_b_f[:], in_=bias_t[:, :, 0])
@@ -149,80 +160,85 @@ def tile_simplemodel_pb_kernel(
         flip_back(1)
         flip_back(2)
 
-        shape = [P, BLOCK_IMAGES, TOKENS, PAIRS, PACK]
         h_of = {}
-        out_t_psum = {}
+        g_of = {}
 
         def pair_sums(block, parity):
             h = h_pool.tile([P, BLOCK_ROWS * PACK], BF16, tag="h", align_bytes=64)
-            tokens = slice(block * BLOCK_IMAGES * TOKENS, (block + 1) * BLOCK_IMAGES * TOKENS)
-            images = slice(block * BLOCK_IMAGES, (block + 1) * BLOCK_IMAGES)
+            first_image = block * BLOCK_IMAGES
+            in_tile = first_image % IMAGES_PER_TILE
+            left = left_psum[first_image // IMAGES_PER_TILE][:].rearrange("p t (b i) -> p b i t", i=TOKENS)
+            vector_shape = [P, VECTOR_IMAGES, TOKENS, PAIRS, PACK]
             nc.vector.tensor_tensor(
-                out=h[:].rearrange("p (b i m t) -> p b i m t", b=BLOCK_IMAGES, i=TOKENS, m=PAIRS),
-                in0=left_t[:, tokens, :].rearrange("p (b i) t -> p b i t", b=BLOCK_IMAGES).unsqueeze(3).to_broadcast(shape),
-                in1=right_t[:, parity, images, :, :].unsqueeze(2).to_broadcast(shape),
+                out=h[:, : VECTOR_IMAGES * IMAGE_COLUMNS].rearrange(
+                    "p (b i m t) -> p b i m t", b=VECTOR_IMAGES, i=TOKENS, m=PAIRS
+                ),
+                in0=left[:, in_tile : in_tile + VECTOR_IMAGES].unsqueeze(3).to_broadcast(vector_shape),
+                in1=right_t[:, parity, first_image : first_image + VECTOR_IMAGES, :, :].unsqueeze(2).to_broadcast(vector_shape),
+                op=ADD,
+            )
+            gpsimd_shape = [P, TOKENS, PAIRS, PACK]
+            nc.gpsimd.tensor_tensor(
+                out=h[:, VECTOR_IMAGES * IMAGE_COLUMNS :].rearrange("p (i m t) -> p i m t", i=TOKENS, m=PAIRS),
+                in0=left_fourth[:, block, :, :].unsqueeze(2).to_broadcast(gpsimd_shape),
+                in1=right_t[:, parity, first_image + VECTOR_IMAGES, :, :].unsqueeze(1).to_broadcast(gpsimd_shape),
                 op=ADD,
             )
             h_of[(block, parity)] = h
 
-        def second_matmul_pass(block, parity):
+        def quantise_pairs(block, parity):
             codes = g_pool.tile([P, BLOCK_ROWS], U32, tag="codes", align_bytes=64)
             scales = g_pool.tile([P, BLOCK_ROWS], U8, tag="scales", align_bytes=64)
             nc.vector.quantize_mx(out=codes[:].bitcast(FP8X4), scales=scales[:], in_=h_of[(block, parity)][:])
-            for c in range(OUT_TILES):
-                if parity == 0:
-                    out_t_psum[c] = psum.tile([P, BLOCK_ROWS], F32, tag="mx", name="out_t_psum%d" % c)
-                weight_columns = cross_words[:, parity, c * PACK * P : (c + 1) * PACK * P]
-                weight_scales = planes[:, HALVES + parity, c * P : (c + 1) * P]
-                if block < BLOCKS - 1:
-                    nc.tensor.matmul_mx(
-                        out=out_t_psum[c][:],
-                        lhsT=weight_columns.bitcast(FP8X4),
-                        lhsT_scale=weight_scales,
-                        rhs=codes[:].bitcast(FP8X4),
-                        rhs_scale=scales[:],
-                        start=(parity == 0),
-                        stop=(parity == HALVES - 1),
-                    )
-                else:
-                    nc.tensor.matmul_mx(
-                        out=out_t_psum[c][:],
-                        lhsT=codes[:, c * P : (c + 1) * P].bitcast(FP8X4),
-                        lhsT_scale=scales[:, c * P : (c + 1) * P],
-                        rhs=cross_words[:, parity, :].bitcast(FP8X4),
-                        rhs_scale=planes[:, HALVES + parity, :],
-                        start=(parity == 0),
-                        stop=(parity == HALVES - 1),
-                    )
+            g_of[(block, parity)] = (codes, scales)
 
-        def finish_last_block(block):
-            result = out_pool.tile([P, BLOCK_IMAGES, EMBED], F32, tag="result")
-            for image in range(BLOCK_IMAGES):
-                nc.vector.tensor_tensor(out=result[:, image, :], in0=out_t_psum[image][:], in1=cross_b_rows[:], op=ADD)
-                first_out_row = (block * BLOCK_IMAGES + image) * P
-                nc.sync.dma_start(out=out_rows[first_out_row : first_out_row + P, :], in_=result[:, image, :])
+        def store_image(block, image, result):
+            first_out_row = (block * BLOCK_IMAGES + image) * P
+            nc.sync.dma_start(out=out_rows[first_out_row : first_out_row + P, :], in_=result[:, image, :])
 
-        def finish_block(block):
+        def second_matmul_by_scalar(block):
             out_t = out_pool.tile([P, OUT_TILES, BLOCK_ROWS], F32, tag="out_t")
             result = out_pool.tile([P, BLOCK_IMAGES, EMBED], F32, tag="result")
-            for first_row in range(0, BLOCK_ROWS, HALF_ROWS):
-                for c in range(OUT_TILES):
-                    nc.scalar.activation(
-                        out=out_t[:, c, first_row : first_row + HALF_ROWS],
-                        in_=out_t_psum[c][:, first_row : first_row + HALF_ROWS],
-                        func=IDENTITY,
-                        bias=cross_b_f[:, c : c + 1],
-                        scale=1.0,
+            for c in range(OUT_TILES):
+                sums = psum_mx.tile([P, BLOCK_ROWS], F32, tag="mx")
+                for parity in range(HALVES):
+                    nc.tensor.matmul_mx(
+                        out=sums[:],
+                        lhsT=cross_words[:, parity, c * PACK * P : (c + 1) * PACK * P].bitcast(FP8X4),
+                        lhsT_scale=planes[:, HALVES + parity, c * P : (c + 1) * P],
+                        rhs=g_of[(block, parity)][0][:].bitcast(FP8X4),
+                        rhs_scale=g_of[(block, parity)][1][:],
+                        start=(parity == 0),
+                        stop=(parity == HALVES - 1),
                     )
+                nc.scalar.activation(
+                    out=out_t[:, c, :], in_=sums[:], func=IDENTITY, bias=cross_b_f[:, c : c + 1], scale=1.0
+                )
             for image in range(BLOCK_IMAGES):
-                rows = psum.tile([P, EMBED], F32, tag="tr")
+                rows = psum_tr.tile([P, EMBED], F32, tag="tr")
                 for c in range(OUT_TILES):
                     nc.tensor.transpose(
                         out=rows[:, c * P : (c + 1) * P], in_=out_t[:, c, image * P : (image + 1) * P], identity=ident[:]
                     )
                 nc.scalar.copy(out=result[:, image, :], in_=rows[:])
-                first_out_row = (block * BLOCK_IMAGES + image) * P
-                nc.sync.dma_start(out=out_rows[first_out_row : first_out_row + P, :], in_=result[:, image, :])
+                store_image(block, image, result)
+
+        def second_matmul_by_vector(block):
+            result = out_pool.tile([P, BLOCK_IMAGES, EMBED], F32, tag="result")
+            for image in range(BLOCK_IMAGES):
+                sums = psum_mx.tile([P, EMBED], F32, tag="mx")
+                for parity in range(HALVES):
+                    nc.tensor.matmul_mx(
+                        out=sums[:],
+                        lhsT=g_of[(block, parity)][0][:, image * P : (image + 1) * P].bitcast(FP8X4),
+                        lhsT_scale=g_of[(block, parity)][1][:, image * P : (image + 1) * P],
+                        rhs=cross_words[:, parity, :].bitcast(FP8X4),
+                        rhs_scale=planes[:, HALVES + parity, :],
+                        start=(parity == 0),
+                        stop=(parity == HALVES - 1),
+                    )
+                nc.vector.tensor_tensor(out=result[:, image, :], in0=sums[:], in1=cross_b_rows[:], op=ADD)
+                store_image(block, image, result)
 
         units = [(block, parity) for block in range(BLOCKS) for parity in range(HALVES)]
         for u in range(len(units) + 1):
@@ -233,9 +249,8 @@ def tile_simplemodel_pb_kernel(
             if u == 1:
                 spread_second_bias()
             if u > 0:
-                second_matmul_pass(units[u - 1][0], units[u - 1][1])
-                if units[u - 1][1] == HALVES - 1:
-                    if units[u - 1][0] < BLOCKS - 1:
-                        finish_block(units[u - 1][0])
-                    else:
-                        finish_last_block(units[u - 1][0])
+                quantise_pairs(units[u - 1][0], units[u - 1][1])
+                if units[u - 1][1] == HALVES - 1 and units[u - 1][0] < BLOCKS - DIRECT_BLOCKS:
+                    second_matmul_by_scalar(units[u - 1][0])
+        for block in range(BLOCKS - DIRECT_BLOCKS, BLOCKS):
+            second_matmul_by_vector(block)

@@ -25,7 +25,7 @@ BLOCK_ROWS = BLOCK_IMAGES * TOKENS * PAIRS
 HALF_ROWS = BLOCK_ROWS // 2
 VECTOR_IMAGES = BLOCK_IMAGES - 1
 IMAGE_COLUMNS = TOKENS * PAIRS * PACK
-DIRECT_BLOCKS = 3
+DIRECT_BLOCKS = 1
 OUT_TILES = EMBED // P
 
 FLOPS = 2 * BATCH * TOKENS * TOKENS * (2 * EMBED) * EMBED + 2 * BATCH * TOKENS * PAIRS * (2 * EMBED) * EMBED
@@ -42,8 +42,9 @@ def tile_simplemodel_pb_kernel(
         keep = ctx.enter_context(tc.tile_pool(name="keep", bufs=1))
         row_pool = ctx.enter_context(tc.tile_pool(name="row_pool", bufs=4))
         h_pool = ctx.enter_context(tc.tile_pool(name="h_pool", bufs=3))
-        g_pool = ctx.enter_context(tc.tile_pool(name="g_pool", bufs=DIRECT_BLOCKS * HALVES))
+        g_pool = ctx.enter_context(tc.tile_pool(name="g_pool", bufs=6))
         out_pool = ctx.enter_context(tc.tile_pool(name="out_pool", bufs=2))
+        image_pool = ctx.enter_context(tc.tile_pool(name="image_pool", bufs=6))
         psum_left = ctx.enter_context(tc.psum_pool(name="psum_left", bufs=TOKEN_TILES))
         psum_mx = ctx.enter_context(tc.psum_pool(name="psum_mx", bufs=3))
         psum_tr = ctx.enter_context(tc.psum_pool(name="psum_tr", bufs=2))
@@ -194,12 +195,15 @@ def tile_simplemodel_pb_kernel(
 
         def store_image(block, image, result):
             first_out_row = (block * BLOCK_IMAGES + image) * P
-            nc.sync.dma_start(out=out_rows[first_out_row : first_out_row + P, :], in_=result[:, image, :])
+            nc.sync.dma_start(out=out_rows[first_out_row : first_out_row + P, :], in_=result[:])
 
-        def second_matmul_by_scalar(block):
-            out_t = out_pool.tile([P, OUT_TILES, BLOCK_ROWS], F32, tag="out_t")
-            result = out_pool.tile([P, BLOCK_IMAGES, EMBED], F32, tag="result")
-            for c in range(OUT_TILES):
+        out_t_of = {}
+
+        def second_matmul_sums(block, out_tiles):
+            if block not in out_t_of:
+                out_t = out_pool.tile([P, OUT_TILES, BLOCK_ROWS], F32, tag="out_t")
+                out_t_of[block] = out_t
+            for c in out_tiles:
                 sums = psum_mx.tile([P, BLOCK_ROWS], F32, tag="mx")
                 for parity in range(HALVES):
                     nc.tensor.matmul_mx(
@@ -212,19 +216,23 @@ def tile_simplemodel_pb_kernel(
                         stop=(parity == HALVES - 1),
                     )
                 nc.scalar.activation(
-                    out=out_t[:, c, :], in_=sums[:], func=IDENTITY, bias=cross_b_f[:, c : c + 1], scale=1.0
+                    out=out_t_of[block][:, c, :], in_=sums[:], func=IDENTITY, bias=cross_b_f[:, c : c + 1], scale=1.0
                 )
-            for image in range(BLOCK_IMAGES):
+
+        def turn_back(block, images):
+            for image in images:
                 rows = psum_tr.tile([P, EMBED], F32, tag="tr")
                 for c in range(OUT_TILES):
                     nc.tensor.transpose(
-                        out=rows[:, c * P : (c + 1) * P], in_=out_t[:, c, image * P : (image + 1) * P], identity=ident[:]
+                        out=rows[:, c * P : (c + 1) * P],
+                        in_=out_t_of[block][:, c, image * P : (image + 1) * P],
+                        identity=ident[:],
                     )
-                nc.scalar.copy(out=result[:, image, :], in_=rows[:])
+                result = image_pool.tile([P, EMBED], F32, tag="result")
+                nc.scalar.copy(out=result[:], in_=rows[:])
                 store_image(block, image, result)
 
         def second_matmul_by_vector(block):
-            result = out_pool.tile([P, BLOCK_IMAGES, EMBED], F32, tag="result")
             for image in range(BLOCK_IMAGES):
                 sums = psum_mx.tile([P, EMBED], F32, tag="mx")
                 for parity in range(HALVES):
@@ -237,20 +245,27 @@ def tile_simplemodel_pb_kernel(
                         start=(parity == 0),
                         stop=(parity == HALVES - 1),
                     )
-                nc.vector.tensor_tensor(out=result[:, image, :], in0=sums[:], in1=cross_b_rows[:], op=ADD)
+                result = image_pool.tile([P, EMBED], F32, tag="result")
+                nc.vector.tensor_tensor(out=result[:], in0=sums[:], in1=cross_b_rows[:], op=ADD)
                 store_image(block, image, result)
 
         units = [(block, parity) for block in range(BLOCKS) for parity in range(HALVES)]
-        for u in range(len(units) + 1):
-            if u < len(units):
-                pair_sums(units[u][0], units[u][1])
-            if 0 < u < TOKEN_TILES:
-                add_first_bias(u)
-            if u == 1:
+        scalar_blocks = BLOCKS - DIRECT_BLOCKS
+        for s in range(len(units) + 2):
+            if s < len(units):
+                pair_sums(units[s][0], units[s][1])
+            if 0 < s < TOKEN_TILES:
+                add_first_bias(s)
+            if s == 1:
                 spread_second_bias()
-            if u > 0:
-                quantise_pairs(units[u - 1][0], units[u - 1][1])
-                if units[u - 1][1] == HALVES - 1 and units[u - 1][0] < BLOCKS - DIRECT_BLOCKS:
-                    second_matmul_by_scalar(units[u - 1][0])
-        for block in range(BLOCKS - DIRECT_BLOCKS, BLOCKS):
-            second_matmul_by_vector(block)
+            if 0 < s <= len(units):
+                quantise_pairs(units[s - 1][0], units[s - 1][1])
+            sums_block, sums_half = divmod(s - 2, 2)
+            if 0 <= sums_block < scalar_blocks:
+                second_matmul_sums(sums_block, (2 * sums_half, 2 * sums_half + 1))
+            if s == len(units):
+                for block in range(scalar_blocks, BLOCKS):
+                    second_matmul_by_vector(block)
+            back_block, back_half = divmod(s - 4, 2)
+            if 0 <= back_block < scalar_blocks:
+                turn_back(back_block, (2 * back_half, 2 * back_half + 1))

@@ -25,7 +25,7 @@ BLOCK_ROWS = BLOCK_IMAGES * TOKENS * PAIRS
 HALF_ROWS = BLOCK_ROWS // 2
 VECTOR_IMAGES = BLOCK_IMAGES - 1
 IMAGE_COLUMNS = TOKENS * PAIRS * PACK
-DIRECT_BLOCKS = 1
+DIRECT_BLOCKS = 2
 OUT_TILES = EMBED // P
 
 FLOPS = 2 * BATCH * TOKENS * TOKENS * (2 * EMBED) * EMBED + 2 * BATCH * TOKENS * PAIRS * (2 * EMBED) * EMBED
@@ -40,7 +40,6 @@ def tile_simplemodel_pb_kernel(
 
     with ExitStack() as ctx:
         keep = ctx.enter_context(tc.tile_pool(name="keep", bufs=1))
-        row_pool = ctx.enter_context(tc.tile_pool(name="row_pool", bufs=4))
         h_pool = ctx.enter_context(tc.tile_pool(name="h_pool", bufs=3))
         g_pool = ctx.enter_context(tc.tile_pool(name="g_pool", bufs=6))
         out_pool = ctx.enter_context(tc.tile_pool(name="out_pool", bufs=2))
@@ -56,42 +55,70 @@ def tile_simplemodel_pb_kernel(
         make_identity(nc, ident[:])
 
         tok_sb = keep.tile([P, TOKEN_TILES, EMBED], BF16)
-        for a in range(TOKEN_TILES):
+        corr_words = keep.tile([P, HALVES, PACK * EMBED], U8, align_bytes=64)
+        cross_words = keep.tile([P, HALVES, PACK * EMBED], U8, align_bytes=64)
+        corr_b_bf = keep.tile([P, PACK], BF16)
+        cross_b_rows_bf = keep.tile([P, EMBED], BF16)
+
+        def load_tokens(a):
             nc.sync.dma_start(out=tok_sb[:, a, :], in_=tok_rows[a * P : (a + 1) * P, :])
 
-        def load_weight(words_dram, scales_dram, words_sb, first_plane):
+        def load_scales(scales_dram, first_plane):
             scale_rows = scales_dram.bitcast(I32).rearrange("g (q r) n -> r q g n", r=4)
             for r in range(4):
                 nc.sync.dma_start(
                     out=planes[r:P:32, first_plane : first_plane + HALVES, :].bitcast(I32), in_=scale_rows[r]
                 )
+
+        def load_words(words_dram, words_sb, half):
             nc.sync.dma_start(
-                out=words_sb[:].bitcast(I32), in_=words_dram.rearrange("g p n t -> p g (n t)").bitcast(I32)
+                out=words_sb[:, half, :].bitcast(I32), in_=words_dram[half].rearrange("p n t -> p (n t)").bitcast(I32)
             )
 
-        corr_words = keep.tile([P, HALVES, PACK * EMBED], U8, align_bytes=64)
-        cross_words = keep.tile([P, HALVES, PACK * EMBED], U8, align_bytes=64)
-        load_weight(corr_w_words, corr_w_scales, corr_words, 0)
-        corr_b_bf = keep.tile([P, PACK], BF16)
+        load_tokens(0)
+        load_scales(corr_w_scales, 0)
         nc.sync.dma_start(out=corr_b_bf[:], in_=corr_b.rearrange("(p t) -> p t", t=PACK))
-        load_weight(cross_w_words, cross_w_scales, cross_words, HALVES)
-        cross_b_rows_bf = keep.tile([P, EMBED], BF16)
+        load_words(corr_w_words, corr_words, 1)
+        load_words(corr_w_words, corr_words, 0)
+        load_tokens(1)
+        load_tokens(2)
+        load_scales(cross_w_scales, HALVES)
+        load_words(cross_w_words, cross_words, 0)
+        load_words(cross_w_words, cross_words, 1)
         nc.sync.dma_start(out=cross_b_rows_bf[:], in_=cross_b.partition_broadcast(P))
 
         tok_grouped = keep.tile([P, TOKEN_TILES, PACK * P], BF16, align_bytes=64)
         tok_codes = keep.tile([P, TOKEN_TILES, P], U32, align_bytes=64)
         tok_scales = keep.tile([P, TOKEN_TILES, P], U8, align_bytes=64)
-        for a in range(TOKEN_TILES):
+
+        def turn_tokens(a):
             pair_words = tok_sb[:, a, :].bitcast(F32)
-            tok_t = psum_tr.tile([P, 2, P], F32, tag="tr")
+            tok_t = psum_mx.tile([P, 2, P], F32, tag="mx")
             for u in range(2):
                 nc.tensor.transpose(out=tok_t[:, u, :], in_=pair_words[:, u : EMBED // 2 : 2], identity=ident[:])
-            nc.vector.tensor_copy(
+            nc.scalar.copy(
                 out=tok_grouped[:, a, :].bitcast(F32).rearrange("p (k u) -> p k u", u=2),
                 in_=tok_t[:].rearrange("p u k -> p k u"),
             )
+
+        def quantise_tokens(a):
             nc.vector.quantize_mx(
                 out=tok_codes[:, a, :].bitcast(FP8X4), scales=tok_scales[:, a, :], in_=tok_grouped[:, a, :]
+            )
+
+        corr_words_by_t = keep.tile([P, HALVES, PACK * EMBED], U8, align_bytes=64)
+        corr_planes_by_t = keep.tile([P, HALVES, EMBED], U8, align_bytes=64)
+
+        def sort_scales(half):
+            nc.vector.tensor_copy(
+                out=corr_planes_by_t[:, half, :].rearrange("p (t m) -> p m t", t=PACK),
+                in_=planes[:, half, :].rearrange("p (m t) -> p m t", t=PACK),
+            )
+
+        def sort_words(half):
+            nc.vector.tensor_copy(
+                out=corr_words_by_t[:, half, :].bitcast(I32).rearrange("p (t m) -> p t m", t=PACK),
+                in_=corr_words[:, half, :].bitcast(I32).rearrange("p (m t) -> p t m", t=PACK),
             )
 
         left_fourth = keep.tile([P, BLOCKS, TOKENS, PACK], F32)
@@ -99,33 +126,23 @@ def tile_simplemodel_pb_kernel(
         corr_b_f = keep.tile([P, PACK], F32)
         cross_b_f = keep.tile([P, OUT_TILES], F32)
         cross_b_rows = keep.tile([P, EMBED], F32)
-        token_rows = {}
         left_psum = {}
         right_psum = {}
 
         def first_matmul(a):
-            for half in range(HALVES):
-                sums = psum_mx.tile([P, EMBED], F32, tag="mx")
-                nc.tensor.matmul_mx(
-                    out=sums[:],
-                    lhsT=tok_codes[:, a, :].bitcast(FP8X4),
-                    lhsT_scale=tok_scales[:, a, :],
-                    rhs=corr_words[:, half, :].bitcast(FP8X4),
-                    rhs_scale=planes[:, half, :],
-                    start=True,
-                    stop=True,
-                )
-                rows = row_pool.tile([P, PACK, P], F32, tag="rows")
-                nc.scalar.copy(out=rows[:], in_=sums[:].rearrange("k (p t) -> k t p", t=PACK))
-                token_rows[(a, half)] = rows
-
-        def flip_back(a):
-            left = psum_left.tile([P, PACK, P], F32, tag="left")
             right = psum_tr.tile([P, PACK, P], F32, tag="tr")
-            for t in range(PACK):
-                nc.tensor.transpose(out=right[:, t, :], in_=token_rows[(a, 1)][:, t, :], identity=ident[:])
-            for t in range(PACK):
-                nc.tensor.transpose(out=left[:, t, :], in_=token_rows[(a, 0)][:, t, :], identity=ident[:])
+            left = psum_left.tile([P, PACK, P], F32, tag="left")
+            for half, sums in ((1, right), (0, left)):
+                for t in range(PACK):
+                    nc.tensor.matmul_mx(
+                        out=sums[:, t, :],
+                        lhsT=corr_words_by_t[:, half, t * PACK * P : (t + 1) * PACK * P].bitcast(FP8X4),
+                        lhsT_scale=corr_planes_by_t[:, half, t * P : (t + 1) * P],
+                        rhs=tok_codes[:, a, :].bitcast(FP8X4),
+                        rhs_scale=tok_scales[:, a, :],
+                        start=True,
+                        stop=True,
+                    )
             left_psum[a] = left
             right_psum[a] = right
             blocks_of_tile = IMAGES_PER_TILE // BLOCK_IMAGES
@@ -135,15 +152,13 @@ def tile_simplemodel_pb_kernel(
             )
 
         def add_first_bias(a):
-            by_parity = right_psum[a][:].rearrange("p t (q j) -> p j q t", j=HALVES)
             images = slice(a * IMAGES_PER_TILE, (a + 1) * IMAGES_PER_TILE)
-            for parity in range(HALVES):
-                nc.vector.tensor_tensor(
-                    out=right_t[:, parity, images, :, :].rearrange("p b m t -> p (b m) t"),
-                    in0=by_parity[:, parity],
-                    in1=corr_b_f[:].unsqueeze(1).to_broadcast([P, IMAGES_PER_TILE * PAIRS, PACK]),
-                    op=ADD,
-                )
+            nc.vector.tensor_tensor(
+                out=right_t[:, :, images, :, :].rearrange("p j b m t -> p j (b m) t"),
+                in0=right_psum[a][:].rearrange("p t (q j) -> p j q t", j=HALVES),
+                in1=corr_b_f[:].unsqueeze(1).unsqueeze(1).to_broadcast([P, HALVES, IMAGES_PER_TILE * PAIRS, PACK]),
+                op=ADD,
+            )
 
         def spread_second_bias():
             nc.scalar.copy(out=cross_b_rows[:], in_=cross_b_rows_bf[:])
@@ -152,14 +167,17 @@ def tile_simplemodel_pb_kernel(
                 nc.tensor.transpose(out=bias_t[:, c, :], in_=cross_b_rows[:, c * P : (c + 1) * P], identity=ident[:])
             nc.scalar.copy(out=cross_b_f[:], in_=bias_t[:, :, 0])
 
+        turn_tokens(0)
+        sort_scales(1)
+        sort_scales(0)
+        quantise_tokens(0)
+        sort_words(1)
+        sort_words(0)
+        nc.scalar.copy(out=corr_b_f[:], in_=corr_b_bf[:])
         first_matmul(0)
-        flip_back(0)
-        nc.vector.tensor_copy(out=corr_b_f[:], in_=corr_b_bf[:])
         add_first_bias(0)
-        first_matmul(1)
-        first_matmul(2)
-        flip_back(1)
-        flip_back(2)
+        turn_tokens(1)
+        turn_tokens(2)
 
         h_of = {}
         g_of = {}
@@ -232,9 +250,14 @@ def tile_simplemodel_pb_kernel(
                 nc.scalar.copy(out=result[:], in_=rows[:])
                 store_image(block, image, result)
 
-        def second_matmul_by_vector(block):
-            for image in range(BLOCK_IMAGES):
-                sums = psum_mx.tile([P, EMBED], F32, tag="mx")
+        direct_sums_of = {}
+
+        def direct_sums(block, images):
+            for image in images:
+                if image < BLOCK_IMAGES // 2:
+                    sums = psum_left.tile([P, EMBED], F32, tag="left")
+                else:
+                    sums = psum_mx.tile([P, EMBED], F32, tag="mx")
                 for parity in range(HALVES):
                     nc.tensor.matmul_mx(
                         out=sums[:],
@@ -245,27 +268,38 @@ def tile_simplemodel_pb_kernel(
                         start=(parity == 0),
                         stop=(parity == HALVES - 1),
                     )
+                direct_sums_of[(block, image)] = sums
+
+        def direct_bias(block, images):
+            for image in images:
                 result = image_pool.tile([P, EMBED], F32, tag="result")
-                nc.vector.tensor_tensor(out=result[:], in0=sums[:], in1=cross_b_rows[:], op=ADD)
+                nc.vector.tensor_tensor(
+                    out=result[:], in0=direct_sums_of[(block, image)][:], in1=cross_b_rows[:], op=ADD
+                )
                 store_image(block, image, result)
 
         units = [(block, parity) for block in range(BLOCKS) for parity in range(HALVES)]
         scalar_blocks = BLOCKS - DIRECT_BLOCKS
-        for s in range(len(units) + 2):
+        for s in range(len(units) + 3):
             if s < len(units):
                 pair_sums(units[s][0], units[s][1])
+            if 1 < s <= TOKEN_TILES:
+                add_first_bias(s - 1)
             if 0 < s < TOKEN_TILES:
-                add_first_bias(s)
+                quantise_tokens(s)
+                first_matmul(s)
             if s == 1:
                 spread_second_bias()
             if 0 < s <= len(units):
                 quantise_pairs(units[s - 1][0], units[s - 1][1])
+            bias_block, bias_half = divmod(s - 3, 2)
+            if scalar_blocks <= bias_block < BLOCKS:
+                direct_bias(bias_block, (2 * bias_half, 2 * bias_half + 1))
             sums_block, sums_half = divmod(s - 2, 2)
             if 0 <= sums_block < scalar_blocks:
                 second_matmul_sums(sums_block, (2 * sums_half, 2 * sums_half + 1))
-            if s == len(units):
-                for block in range(scalar_blocks, BLOCKS):
-                    second_matmul_by_vector(block)
+            if scalar_blocks <= sums_block < BLOCKS:
+                direct_sums(sums_block, (2 * sums_half, 2 * sums_half + 1))
             back_block, back_half = divmod(s - 4, 2)
             if 0 <= back_block < scalar_blocks:
                 turn_back(back_block, (2 * back_half, 2 * back_half + 1))

from contextlib import ExitStack

import concourse.mybir as mybir
from concourse.masks import make_identity

F32 = mybir.dt.float32
BF16 = mybir.dt.bfloat16
I32 = mybir.dt.int32
U32 = mybir.dt.uint32
U8 = mybir.dt.uint8
FP8X4 = mybir.dt.float8_e4m3fn_x4
ADD = mybir.AluOpType.add
IDENTITY = mybir.ActivationFunctionType.Identity

P = 128
PACK = 4
BATCH, TOKENS, EMBED = 24, 16, 512
PAIRS = TOKENS // 2
HALVES = 2
TOKEN_TILES = BATCH * TOKENS // P
IMAGES_PER_TILE = P // TOKENS
BLOCK_IMAGES = 4
BLOCKS = BATCH // BLOCK_IMAGES
BLOCK_ROWS = BLOCK_IMAGES * TOKENS * PAIRS
HALF_ROWS = BLOCK_ROWS // 2
VECTOR_IMAGES = BLOCK_IMAGES - 1
IMAGE_COLUMNS = TOKENS * PAIRS * PACK
DIRECT_BLOCKS = 2
OUT_TILES = EMBED // P

FLOPS = 2 * BATCH * TOKENS * TOKENS * (2 * EMBED) * EMBED + 2 * BATCH * TOKENS * PAIRS * (2 * EMBED) * EMBED


def tile_simplemodel_pb_kernel(
    tc, tok, corr_w_words, corr_w_scales, corr_b, cross_w_words, cross_w_scales, cross_b, out
):
    nc = tc.nc
    tok_rows = tok.rearrange("b i e -> (b i) e")
    out_rows = out.rearrange("b i m n -> (b i m) n")

    with ExitStack() as ctx:
        keep = ctx.enter_context(tc.tile_pool(name="keep", bufs=1))
        h_pool = ctx.enter_context(tc.tile_pool(name="h_pool", bufs=3))
        g_pool = ctx.enter_context(tc.tile_pool(name="g_pool", bufs=6))
        out_pool = ctx.enter_context(tc.tile_pool(name="out_pool", bufs=2))
        image_pool = ctx.enter_context(tc.tile_pool(name="image_pool", bufs=6))
        psum_left = ctx.enter_context(tc.psum_pool(name="psum_left", bufs=TOKEN_TILES))
        psum_mx = ctx.enter_context(tc.psum_pool(name="psum_mx", bufs=3))
        psum_tr = ctx.enter_context(tc.psum_pool(name="psum_tr", bufs=2))
        ctx.enter_context(tc.manual_schedule())

        planes = keep.tile([P, 2 * HALVES, EMBED], U8, align_bytes=64)
        nc.vector.memset(planes[:].bitcast(I32), 0)
        ident = keep.tile([P, P], F32)
        make_identity(nc, ident[:])

        tok_sb = keep.tile([P, TOKEN_TILES, EMBED], BF16)
        corr_words = keep.tile([P, HALVES, PACK * EMBED], U8, align_bytes=64)
        cross_words = keep.tile([P, HALVES, PACK * EMBED], U8, align_bytes=64)
        corr_b_bf = keep.tile([P, PACK], BF16)
        cross_b_rows_bf = keep.tile([P, EMBED], BF16)

        def load_tokens(a):
            nc.sync.dma_start(out=tok_sb[:, a, :], in_=tok_rows[a * P : (a + 1) * P, :])

        def load_scales(scales_dram, first_plane):
            scale_rows = scales_dram.bitcast(I32).rearrange("g (q r) n -> r q g n", r=4)
            for r in range(4):
                nc.sync.dma_start(
                    out=planes[r:P:32, first_plane : first_plane + HALVES, :].bitcast(I32), in_=scale_rows[r]
                )

        def load_words(words_dram, words_sb, half):
            nc.sync.dma_start(
                out=words_sb[:, half, :].bitcast(I32), in_=words_dram[half].rearrange("p n t -> p (n t)").bitcast(I32)
            )

        load_tokens(0)
        load_scales(corr_w_scales, 0)
        nc.sync.dma_start(out=corr_b_bf[:], in_=corr_b.rearrange("(p t) -> p t", t=PACK))
        load_words(corr_w_words, corr_words, 1)
        load_words(corr_w_words, corr_words, 0)
        load_tokens(1)
        load_tokens(2)
        load_scales(cross_w_scales, HALVES)
        load_words(cross_w_words, cross_words, 0)
        load_words(cross_w_words, cross_words, 1)
        nc.sync.dma_start(out=cross_b_rows_bf[:], in_=cross_b.partition_broadcast(P))

        tok_grouped = keep.tile([P, TOKEN_TILES, PACK * P], BF16, align_bytes=64)
        tok_codes = keep.tile([P, TOKEN_TILES, P], U32, align_bytes=64)
        tok_scales = keep.tile([P, TOKEN_TILES, P], U8, align_bytes=64)

        def turn_tokens(a):
            pair_words = tok_sb[:, a, :].bitcast(F32)
            tok_t = psum_mx.tile([P, 2, P], F32, tag="mx")
            for u in range(2):
                nc.tensor.transpose(out=tok_t[:, u, :], in_=pair_words[:, u : EMBED // 2 : 2], identity=ident[:])
            nc.scalar.copy(
                out=tok_grouped[:, a, :].bitcast(F32).rearrange("p (k u) -> p k u", u=2),
                in_=tok_t[:].rearrange("p u k -> p k u"),
            )

        def quantise_tokens(a):
            nc.vector.quantize_mx(
                out=tok_codes[:, a, :].bitcast(FP8X4), scales=tok_scales[:, a, :], in_=tok_grouped[:, a, :]
            )

        corr_words_by_t = keep.tile([P, HALVES, PACK * EMBED], U8, align_bytes=64)
        corr_planes_by_t = keep.tile([P, HALVES, EMBED], U8, align_bytes=64)

        def sort_scales(half):
            nc.vector.tensor_copy(
                out=corr_planes_by_t[:, half, :].rearrange("p (t m) -> p m t", t=PACK),
                in_=planes[:, half, :].rearrange("p (m t) -> p m t", t=PACK),
            )

        def sort_words(half):
            nc.vector.tensor_copy(
                out=corr_words_by_t[:, half, :].bitcast(I32).rearrange("p (t m) -> p t m", t=PACK),
                in_=corr_words[:, half, :].bitcast(I32).rearrange("p (m t) -> p t m", t=PACK),
            )

        left_fourth = keep.tile([P, BLOCKS, TOKENS, PACK], F32)
        right_t = keep.tile([P, HALVES, BATCH, PAIRS, PACK], F32)
        corr_b_f = keep.tile([P, PACK], F32)
        cross_b_f = keep.tile([P, OUT_TILES], F32)
        cross_b_rows = keep.tile([P, EMBED], F32)
        left_psum = {}
        right_psum = {}

        def first_matmul(a):
            right = psum_tr.tile([P, PACK, P], F32, tag="tr")
            left = psum_left.tile([P, PACK, P], F32, tag="left")
            for half, sums in ((1, right), (0, left)):
                for t in range(PACK):
                    nc.tensor.matmul_mx(
                        out=sums[:, t, :],
                        lhsT=corr_words_by_t[:, half, t * PACK * P : (t + 1) * PACK * P].bitcast(FP8X4),
                        lhsT_scale=corr_planes_by_t[:, half, t * P : (t + 1) * P],
                        rhs=tok_codes[:, a, :].bitcast(FP8X4),
                        rhs_scale=tok_scales[:, a, :],
                        start=True,
                        stop=True,
                    )
            left_psum[a] = left
            right_psum[a] = right
            blocks_of_tile = IMAGES_PER_TILE // BLOCK_IMAGES
            nc.scalar.copy(
                out=left_fourth[:, a * blocks_of_tile : (a + 1) * blocks_of_tile, :, :],
                in_=left[:].rearrange("p t (b i) -> p b i t", i=TOKENS)[:, VECTOR_IMAGES:IMAGES_PER_TILE:BLOCK_IMAGES],
            )

        def add_first_bias(a):
            images = slice(a * IMAGES_PER_TILE, (a + 1) * IMAGES_PER_TILE)
            nc.vector.tensor_tensor(
                out=right_t[:, :, images, :, :].rearrange("p j b m t -> p j (b m) t"),
                in0=right_psum[a][:].rearrange("p t (q j) -> p j q t", j=HALVES),
                in1=corr_b_f[:].unsqueeze(1).unsqueeze(1).to_broadcast([P, HALVES, IMAGES_PER_TILE * PAIRS, PACK]),
                op=ADD,
            )

        def spread_second_bias():
            nc.scalar.copy(out=cross_b_rows[:], in_=cross_b_rows_bf[:])
            bias_t = psum_tr.tile([P, OUT_TILES, P], F32, tag="tr")
            for c in range(OUT_TILES):
                nc.tensor.transpose(out=bias_t[:, c, :], in_=cross_b_rows[:, c * P : (c + 1) * P], identity=ident[:])
            nc.scalar.copy(out=cross_b_f[:], in_=bias_t[:, :, 0])

        turn_tokens(0)
        sort_scales(1)
        sort_scales(0)
        quantise_tokens(0)
        sort_words(1)
        sort_words(0)
        nc.scalar.copy(out=corr_b_f[:], in_=corr_b_bf[:])
        first_matmul(0)
        add_first_bias(0)
        turn_tokens(1)
        turn_tokens(2)

        h_of = {}
        g_of = {}

        def pair_sums(block, parity):
            h = h_pool.tile([P, BLOCK_ROWS * PACK], BF16, tag="h", align_bytes=64)
            first_image = block * BLOCK_IMAGES
            in_tile = first_image % IMAGES_PER_TILE
            left = left_psum[first_image // IMAGES_PER_TILE][:].rearrange("p t (b i) -> p b i t", i=TOKENS)
            vector_shape = [P, VECTOR_IMAGES, TOKENS, PAIRS, PACK]
            nc.vector.tensor_tensor(
                out=h[:, : VECTOR_IMAGES * IMAGE_COLUMNS].rearrange(
                    "p (b i m t) -> p b i m t", b=VECTOR_IMAGES, i=TOKENS, m=PAIRS
                ),
                in0=left[:, in_tile : in_tile + VECTOR_IMAGES].unsqueeze(3).to_broadcast(vector_shape),
                in1=right_t[:, parity, first_image : first_image + VECTOR_IMAGES, :, :].unsqueeze(2).to_broadcast(vector_shape),
                op=ADD,
            )
            gpsimd_shape = [P, TOKENS, PAIRS, PACK]
            nc.gpsimd.tensor_tensor(
                out=h[:, VECTOR_IMAGES * IMAGE_COLUMNS :].rearrange("p (i m t) -> p i m t", i=TOKENS, m=PAIRS),
                in0=left_fourth[:, block, :, :].unsqueeze(2).to_broadcast(gpsimd_shape),
                in1=right_t[:, parity, first_image + VECTOR_IMAGES, :, :].unsqueeze(1).to_broadcast(gpsimd_shape),
                op=ADD,
            )
            h_of[(block, parity)] = h

        def quantise_pairs(block, parity):
            codes = g_pool.tile([P, BLOCK_ROWS], U32, tag="codes", align_bytes=64)
            scales = g_pool.tile([P, BLOCK_ROWS], U8, tag="scales", align_bytes=64)
            nc.vector.quantize_mx(out=codes[:].bitcast(FP8X4), scales=scales[:], in_=h_of[(block, parity)][:])
            g_of[(block, parity)] = (codes, scales)

        def store_image(block, image, result):
            first_out_row = (block * BLOCK_IMAGES + image) * P
            nc.sync.dma_start(out=out_rows[first_out_row : first_out_row + P, :], in_=result[:])

        out_t_of = {}

        def second_matmul_sums(block, out_tiles):
            if block not in out_t_of:
                out_t = out_pool.tile([P, OUT_TILES, BLOCK_ROWS], F32, tag="out_t")
                out_t_of[block] = out_t
            for c in out_tiles:
                sums = psum_mx.tile([P, BLOCK_ROWS], F32, tag="mx")
                for parity in range(HALVES):
                    nc.tensor.matmul_mx(
                        out=sums[:],
                        lhsT=cross_words[:, parity, c * PACK * P : (c + 1) * PACK * P].bitcast(FP8X4),
                        lhsT_scale=planes[:, HALVES + parity, c * P : (c + 1) * P],
                        rhs=g_of[(block, parity)][0][:].bitcast(FP8X4),
                        rhs_scale=g_of[(block, parity)][1][:],
                        start=(parity == 0),
                        stop=(parity == HALVES - 1),
                    )
                nc.scalar.activation(
                    out=out_t_of[block][:, c, :], in_=sums[:], func=IDENTITY, bias=cross_b_f[:, c : c + 1], scale=1.0
                )

        def turn_back(block, images):
            for image in images:
                rows = psum_tr.tile([P, EMBED], F32, tag="tr")
                for c in range(OUT_TILES):
                    nc.tensor.transpose(
                        out=rows[:, c * P : (c + 1) * P],
                        in_=out_t_of[block][:, c, image * P : (image + 1) * P],
                        identity=ident[:],
                    )
                result = image_pool.tile([P, EMBED], F32, tag="result")
                nc.scalar.copy(out=result[:], in_=rows[:])
                store_image(block, image, result)

        direct_sums_of = {}

        def direct_sums(block, images):
            for image in images:
                if image < BLOCK_IMAGES // 2:
                    sums = psum_left.tile([P, EMBED], F32, tag="left")
                else:
                    sums = psum_mx.tile([P, EMBED], F32, tag="mx")
                for parity in range(HALVES):
                    nc.tensor.matmul_mx(
                        out=sums[:],
                        lhsT=g_of[(block, parity)][0][:, image * P : (image + 1) * P].bitcast(FP8X4),
                        lhsT_scale=g_of[(block, parity)][1][:, image * P : (image + 1) * P],
                        rhs=cross_words[:, parity, :].bitcast(FP8X4),
                        rhs_scale=planes[:, HALVES + parity, :],
                        start=(parity == 0),
                        stop=(parity == HALVES - 1),
                    )
                direct_sums_of[(block, image)] = sums

        def direct_bias(block, images):
            for image in images:
                result = image_pool.tile([P, EMBED], F32, tag="result")
                nc.vector.tensor_tensor(
                    out=result[:], in0=direct_sums_of[(block, image)][:], in1=cross_b_rows[:], op=ADD
                )
                store_image(block, image, result)

        units = [(block, parity) for block in range(BLOCKS) for parity in range(HALVES)]
        scalar_blocks = BLOCKS - DIRECT_BLOCKS
        for s in range(len(units) + 3):
            if s < len(units):
                pair_sums(units[s][0], units[s][1])
            if 1 < s <= TOKEN_TILES:
                add_first_bias(s - 1)
            if 0 < s < TOKEN_TILES:
                quantise_tokens(s)
                first_matmul(s)
            if s == 1:
                spread_second_bias()
            if 0 < s <= len(units):
                quantise_pairs(units[s - 1][0], units[s - 1][1])
            bias_block, bias_half = divmod(s - 3, 2)
            if scalar_blocks <= bias_block < BLOCKS:
                direct_bias(bias_block, (2 * bias_half, 2 * bias_half + 1))
            sums_block, sums_half = divmod(s - 2, 2)
            if 0 <= sums_block < scalar_blocks:
                second_matmul_sums(sums_block, (2 * sums_half, 2 * sums_half + 1))
            if scalar_blocks <= sums_block < BLOCKS:
                direct_sums(sums_block, (2 * sums_half, 2 * sums_half + 1))
            back_block, back_half = divmod(s - 4, 2)
            if 0 <= back_block < scalar_blocks:
                turn_back(back_block, (2 * back_half, 2 * back_half + 1))
